import numpy as np
import ml_dtypes


def mxq(x, axis, fmt="e4m3"):
    dtype, down = {"e4m3": (ml_dtypes.float8_e4m3fn, 7), "e5m2": (ml_dtypes.float8_e5m2, 14)}[fmt]
    v = np.moveaxis(np.asarray(x, np.float32).astype(ml_dtypes.bfloat16).astype(np.float64), axis, -1)
    blocks = v.reshape(v.shape[:-1] + (-1, 32))
    amax = np.abs(blocks).max(-1, keepdims=True)
    byte = np.maximum(np.where(amax > 0, np.frexp(amax)[1] - 1 + 127, 0) - down, 1)
    scale = np.exp2(byte - 127.0)
    codes = (blocks / scale).astype(np.float32).astype(dtype).astype(np.float64)
    return np.moveaxis((codes * scale).reshape(v.shape), -1, axis)


WIDE = False


def mx_kscale(k):
    if not WIDE:
        return np.ones(k)
    levels = np.array([10, -10, 5, -5, 0])
    a = np.random.permutation(np.resize(levels, k // 512 * 4)).reshape(k // 512, 4)
    idx = np.arange(k)
    return np.exp2(a[idx // 512, idx % 128 // 32])


BF16 = ml_dtypes.bfloat16


def bf(x):
    return np.asarray(x, np.float32).astype(BF16)


def f64(x):
    return np.asarray(x).astype(np.float64)


E2M1 = np.array([0.0, 0.5, 1.0, 1.5, 2.0, 3.0, 4.0, 6.0, -0.0, -0.5, -1.0, -1.5, -2.0, -3.0, -4.0, -6.0])


def pack_weight(w, fmt):
    k, n = w.shape
    w = f64(bf(w)).reshape(k // 32, 32, n)
    amax = np.abs(w).max(1)
    if fmt == "e4m3":
        byte = np.frexp(amax)[1] - 1 + 127 - 7
    else:
        mant, ex = np.frexp(amax / 6.0)
        byte = np.where(mant > 0.5, ex, ex - 1) + 127
    byte = np.clip(np.where(amax > 0, byte, 1), 1, 254)
    scaled = (w * np.exp2(127.0 - byte)[:, None, :]).reshape(k, n).astype(np.float32)
    by_word = np.ascontiguousarray(scaled.reshape(k // 512, 128, 4, n).transpose(0, 1, 3, 2))
    if fmt == "e4m3":
        words = by_word.astype(ml_dtypes.float8_e4m3fn).view(np.uint8)
    else:
        c = by_word.astype(ml_dtypes.float4_e2m1fn).view(np.uint8) & 0xF
        words = c[..., 0::2] | (c[..., 1::2] << 4)
    return np.ascontiguousarray(words), np.ascontiguousarray(byte.astype(np.uint8).reshape(k // 512, 16, n))


def unpack_weight(words, scales, fmt):
    g, p, n, _ = words.shape
    if fmt == "e4m3":
        vals = np.ascontiguousarray(words).view(ml_dtypes.float8_e4m3fn).astype(np.float64)
    else:
        nib = np.empty((g, p, n, 4), np.uint8)
        nib[..., 0::2] = words & 0xF
        nib[..., 1::2] = words >> 4
        vals = E2M1[nib]
    vals = vals * np.repeat(np.exp2(scales.astype(np.float64) - 127.0), 8, axis=1)[..., None]
    return vals.transpose(0, 1, 3, 2).reshape(g * 512, n)


B, G, Z1, Z2, H, PD = 256, 16, 256, 256, 512, 512
CIN = Z1 + Z2


def glin(x, Wk, b):
    y = mxq(x, 2, "e4m3").transpose(1, 0, 2) @ Wk
    return y.transpose(1, 0, 2) + f64(b)


def setup_inputs():
    s = mx_kscale(CIN)
    z1 = bf((np.random.standard_normal((B, G, Z1)) * s[:Z1]).reshape(B, G * Z1))
    z2 = bf((np.random.standard_normal((B, G, Z2)) * s[Z1:]).reshape(B, G * Z2))
    W1 = np.random.standard_normal((G, H, CIN)) / np.sqrt(CIN) / s
    W1_words, W1_scales = pack_weight(np.ascontiguousarray(W1.swapaxes(1, 2)).reshape(-1, H), "e4m3")
    b1 = bf(np.random.standard_normal((G, H)) * 0.2)
    W2 = np.random.standard_normal((G, H, H)) * 1.4 / np.sqrt(H)
    W2_words, W2_scales = pack_weight(np.ascontiguousarray(W2.swapaxes(1, 2)).reshape(-1, H), "e4m3")
    b2 = bf(np.random.standard_normal((G, H)) * 0.2)
    return {"z1": z1,
            "z2": z2,
            "W1_words": W1_words,
            "W1_scales": W1_scales,
            "b1": b1,
            "W2_words": W2_words,
            "W2_scales": W2_scales,
            "b2": b2}


def reference(z1, z2, W1_words, W1_scales, b1, W2_words, W2_scales, b2):
    z = np.concatenate([f64(z1).reshape(B, G, Z1), f64(z2).reshape(B, G, Z2)], axis=2)
    h1 = np.maximum(glin(z, unpack_weight(W1_words, W1_scales, "e4m3").reshape(G, CIN, H), b1), 0.0)
    return np.maximum(glin(h1, unpack_weight(W2_words, W2_scales, "e4m3").reshape(G, H, H), b2), 0.0) + h1

@@ -1,0 +1,217 @@
+from contextlib import ExitStack
+
+import concourse.mybir as mybir
+from concourse.masks import make_identity
+
+F32 = mybir.dt.float32
+BF16 = mybir.dt.bfloat16
+I32 = mybir.dt.int32
+U32 = mybir.dt.uint32
+U8 = mybir.dt.uint8
+FP8X4 = mybir.dt.float8_e4m3fn_x4
+RELU = mybir.ActivationFunctionType.Relu
+ADD = mybir.AluOpType.add
+MAX = mybir.AluOpType.max
+
+P = 128
+PACK = 4
+BATCH = 256
+ROW_TILES = BATCH // P
+CODES = 16
+HALF = 256
+WIDTH = 512
+COL_TILES = WIDTH // P
+PLANES = 4
+LOAD_CODES = 2
+
+FLOPS = 2 * 2 * BATCH * CODES * WIDTH * WIDTH
+
+LAG_LAYER1 = 1
+LAG_HIDDEN = 2
+LAG_LAYER2 = 3
+LAG_FINISH = 4
+
+
+def tile_linearwdecoder_pa_e_kernel(tc, z1, z2, W1_words, W1_scales, b1, W2_words, W2_scales, b2, out):
+    nc = tc.nc
+    with ExitStack() as stack:
+        resident = stack.enter_context(tc.tile_pool(name="resident", bufs=1))
+        work = stack.enter_context(tc.tile_pool(name="work", bufs=3))
+        banks = stack.enter_context(tc.psum_pool(name="banks", bufs=8))
+        stack.enter_context(tc.manual_schedule())
+
+        z_rows = resident.tile([P, ROW_TILES, CODES, WIDTH], BF16)
+        w1_words = resident.tile([P, CODES, WIDTH], U32, align_bytes=64)
+        w2_words = resident.tile([P, CODES, WIDTH], U32, align_bytes=64)
+        w1_planes = resident.tile([P, CODES // PLANES, WIDTH], U8, align_bytes=64)
+        w2_planes = resident.tile([P, CODES // PLANES, WIDTH], U8, align_bytes=64)
+        b1_rows = resident.tile([P, CODES, WIDTH], BF16)
+        b2_raw = resident.tile([P, P], BF16)
+        b2_f32 = resident.tile([P, P], F32)
+        b2_cols = resident.tile([P, CODES * COL_TILES], F32)
+        ident = resident.tile([P, P], F32)
+
+        nc.vector.memset(w1_planes[:].rearrange("p a n -> p (a n)").bitcast(I32), 0)
+        nc.vector.memset(w2_planes[:].rearrange("p a n -> p (a n)").bitcast(I32), 0)
+        nc.vector.memset(b2_f32[:], 0.0)
+        make_identity(nc, ident[:])
+
+        nc.sync.dma_start(out=b2_raw[0 : CODES * COL_TILES, :], in_=b2.rearrange("g (j m) -> (g j) m", m=P))
+
+        def load_planes(planes, scales, a):
+            for quadrant in range(4):
+                nc.sync.dma_start(
+                    out=planes[32 * quadrant : 32 * quadrant + 4 * PLANES, a, :].bitcast(I32),
+                    in_=scales[PLANES * a : PLANES * (a + 1), 4 * quadrant : 4 * quadrant + 4, :].bitcast(I32),
+                )
+
+        def load_words(words, packed, codes):
+            nc.sync.dma_start(
+                out=words[:, codes, :].bitcast(I32),
+                in_=packed[codes].rearrange("g p n t -> p g (n t)").bitcast(I32),
+            )
+
+        for c in range(CODES // LOAD_CODES):
+            codes = slice(c * LOAD_CODES, (c + 1) * LOAD_CODES)
+            cols = slice(c * LOAD_CODES * HALF, (c + 1) * LOAD_CODES * HALF)
+            for r in range(ROW_TILES):
+                rows = slice(r * P, (r + 1) * P)
+                nc.sync.dma_start(out=z_rows[:, r, codes, 0:HALF], in_=z1[rows, cols].rearrange("p (g k) -> p g k", k=HALF))
+                nc.sync.dma_start(out=z_rows[:, r, codes, HALF:WIDTH], in_=z2[rows, cols].rearrange("p (g k) -> p g k", k=HALF))
+            if (c * LOAD_CODES) % PLANES == 0:
+                load_planes(w1_planes, W1_scales, c * LOAD_CODES // PLANES)
+            load_words(w1_words, W1_words, codes)
+            nc.sync.dma_start(
+                out=b1_rows[:, codes, :].rearrange("p g n -> p (g n)"),
+                in_=b1[codes, :].rearrange("g n -> (g n)").partition_broadcast(P),
+            )
+            if (c * LOAD_CODES) % PLANES == 0:
+                load_planes(w2_planes, W2_scales, c * LOAD_CODES // PLANES)
+            load_words(w2_words, W2_words, codes)
+
+        nc.vector.tensor_copy(out=b2_f32[0 : CODES * COL_TILES, :], in_=b2_raw[0 : CODES * COL_TILES, :])
+        b2_bank = banks.tile([P, WIDTH], F32, tag="bank")
+        nc.tensor.transpose(b2_bank[:, 0:P], b2_f32[:], ident[:])
+        nc.vector.tensor_copy(out=b2_cols[:], in_=b2_bank[:, 0 : CODES * COL_TILES])
+
+        z_words = z_rows[:].bitcast(F32)
+        kept = {}
+
+        def plane_of(planes, g):
+            return planes[4 * (g % PLANES) : P, g // PLANES, :]
+
+        def quantise_z(g):
+            z_bank = banks.tile([P, 2, BATCH], F32, tag="bank")
+            for r in range(ROW_TILES):
+                for u in range(2):
+                    nc.tensor.transpose(z_bank[:, u, r * P : (r + 1) * P], z_words[:, r, g, u : HALF : 2], ident[:])
+            z_grouped = work.tile([P, BATCH, PACK], BF16, align_bytes=64)
+            nc.scalar.copy(out=z_grouped[:].bitcast(F32), in_=z_bank[:].rearrange("p u b -> p b u"))
+            z_codes = work.tile([P, BATCH], U32, align_bytes=64)
+            z_scales = work.tile([P, BATCH], U8, align_bytes=64)
+            nc.vector.quantize_mx(
+                out=z_codes[:].bitcast(FP8X4), scales=z_scales[:], in_=z_grouped[:].rearrange("p b t -> p (b t)")
+            )
+            kept["z", g] = (z_codes, z_scales)
+
+        def layer1(g):
+            z_codes, z_scales = kept["z", g]
+            pre = work.tile([P, ROW_TILES, PACK, P], F32, bufs=6)
+            for r in range(ROW_TILES):
+                rows = slice(r * P, (r + 1) * P)
+                acc1 = banks.tile([P, WIDTH], F32, tag="bank")
+                nc.tensor.matmul_mx(
+                    out=acc1[:],
+                    lhsT=z_codes[:, rows].bitcast(FP8X4),
+                    lhsT_scale=z_scales[:, rows],
+                    rhs=w1_words[:, g, :].bitcast(FP8X4),
+                    rhs_scale=plane_of(w1_planes, g),
+                    start=True,
+                    stop=True,
+                )
+                nc.vector.tensor_tensor(
+                    out=pre[:, r, :, :],
+                    in0=acc1[:].rearrange("b (m t) -> b t m", t=PACK),
+                    in1=b1_rows[:, g, :].rearrange("b (m t) -> b t m", t=PACK),
+                    op=ADD,
+                )
+            kept["pre", g] = pre
+
+        def transpose_hidden(g):
+            pre = kept["pre", g]
+            h_grouped = work.tile([P, BATCH, PACK], BF16, align_bytes=64)
+            for r in range(ROW_TILES):
+                h_bank = banks.tile([P, PACK, P], F32, tag="bank")
+                for t in range(PACK):
+                    nc.tensor.transpose(h_bank[:, t, :], pre[:, r, t, :], ident[:])
+                nc.scalar.activation(
+                    out=h_grouped[:, r * P : (r + 1) * P, :], in_=h_bank[:].rearrange("p t b -> p b t"), func=RELU
+                )
+            kept["h_grouped", g] = h_grouped
+
+        def quantise_hidden(g):
+            h_grouped = kept["h_grouped", g]
+            h_codes = work.tile([P, BATCH], U32, align_bytes=64)
+            h_scales = work.tile([P, BATCH], U8, align_bytes=64)
+            nc.vector.quantize_mx(
+                out=h_codes[:].bitcast(FP8X4), scales=h_scales[:], in_=h_grouped[:].rearrange("p b t -> p (b t)")
+            )
+            kept["h", g] = (h_codes, h_scales)
+
+        def layer2(g):
+            h_codes, h_scales = kept["h", g]
+            branch = work.tile([P, COL_TILES, BATCH], F32)
+            for half in range(COL_TILES // 2):
+                acc2 = banks.tile([P, 2, BATCH], F32, tag="bank")
+                for i in range(2):
+                    j = 2 * half + i
+                    nc.tensor.matmul_mx(
+                        out=acc2[:, i, :],
+                        lhsT=w2_words[:, g, j * P : (j + 1) * P].bitcast(FP8X4),
+                        lhsT_scale=plane_of(w2_planes, g)[:, j * P : (j + 1) * P],
+                        rhs=h_codes[:].bitcast(FP8X4),
+                        rhs_scale=h_scales[:],
+                        start=True,
+                        stop=True,
+                    )
+                for i in range(2):
+                    j = 2 * half + i
+                    nc.scalar.activation(
+                        out=branch[:, j, :],
+                        in_=acc2[:, i, :],
+                        func=RELU,
+                        bias=b2_cols[:, COL_TILES * g + j : COL_TILES * g + j + 1],
+                    )
+            kept["branch", g] = branch
+
+        def finish(g):
+            branch = kept["branch", g]
+            pre = kept["pre", g]
+            result = work.tile([P, ROW_TILES, WIDTH], F32, bufs=4)
+            for r in range(ROW_TILES):
+                back = banks.tile([P, WIDTH], F32, tag="bank")
+                for j in range(COL_TILES):
+                    nc.tensor.transpose(back[:, j * P : (j + 1) * P], branch[:, j, r * P : (r + 1) * P], ident[:])
+                nc.vector.scalar_tensor_tensor(
+                    out=result[:, r, :].rearrange("b (m t) -> b m t", t=PACK),
+                    in0=pre[:, r, :, :].rearrange("b t m -> b m t"),
+                    scalar=0.0,
+                    in1=back[:].rearrange("b (m t) -> b m t", t=PACK),
+                    op0=MAX,
+                    op1=ADD,
+                )
+            nc.gpsimd.dma_start(out=out.rearrange("(r p) g n -> p r g n", p=P)[:, :, g, :], in_=result[:])
+
+        for round_no in range(CODES + LAG_FINISH):
+            if round_no < CODES:
+                quantise_z(round_no)
+            if 0 <= round_no - LAG_HIDDEN < CODES:
+                transpose_hidden(round_no - LAG_HIDDEN)
+            if 0 <= round_no - LAG_FINISH < CODES:
+                finish(round_no - LAG_FINISH)
+            if 0 <= round_no - LAG_LAYER1 < CODES:
+                layer1(round_no - LAG_LAYER1)
+            if 0 <= round_no - LAG_HIDDEN < CODES:
+                quantise_hidden(round_no - LAG_HIDDEN)
+            if 0 <= round_no - LAG_LAYER2 < CODES:
+                layer2(round_no - LAG_LAYER2)

@@ -45,7 +45,9 @@ def tile_linearwdecoder_pa_e_kernel(tc, z1, z2, W1_words, W1_scales, b1, W2_word
         w2_words = resident.tile([P, CODES, WIDTH], U32, align_bytes=64)
         w1_planes = resident.tile([P, CODES // PLANES, WIDTH], U8, align_bytes=64)
         w2_planes = resident.tile([P, CODES // PLANES, WIDTH], U8, align_bytes=64)
+        b1_small = resident.tile([P, WIDTH], BF16)
         b1_rows = resident.tile([P, CODES, WIDTH], BF16)
+        ident_bf16 = resident.tile([P, P], BF16)
         b2_raw = resident.tile([P, P], BF16)
         b2_f32 = resident.tile([P, P], F32)
         b2_cols = resident.tile([P, CODES * COL_TILES], F32)
@@ -54,8 +56,11 @@ def tile_linearwdecoder_pa_e_kernel(tc, z1, z2, W1_words, W1_scales, b1, W2_word
         nc.vector.memset(w1_planes[:].rearrange("p a n -> p (a n)").bitcast(I32), 0)
         nc.vector.memset(w2_planes[:].rearrange("p a n -> p (a n)").bitcast(I32), 0)
         nc.vector.memset(b2_f32[:], 0.0)
+        nc.vector.memset(b1_small[:], 0.0)
+        make_identity(nc, ident_bf16[:])
         make_identity(nc, ident[:])
 
+        nc.sync.dma_start(out=b1_small[0:CODES, :], in_=b1)
         nc.sync.dma_start(out=b2_raw[0 : CODES * COL_TILES, :], in_=b2.rearrange("g (j m) -> (g j) m", m=P))
 
         def load_planes(planes, scales, a):
@@ -81,10 +86,6 @@ def tile_linearwdecoder_pa_e_kernel(tc, z1, z2, W1_words, W1_scales, b1, W2_word
             if (c * LOAD_CODES) % PLANES == 0:
                 load_planes(w1_planes, W1_scales, c * LOAD_CODES // PLANES)
             load_words(w1_words, W1_words, codes)
-            nc.sync.dma_start(
-                out=b1_rows[:, codes, :].rearrange("p g n -> p (g n)"),
-                in_=b1[codes, :].rearrange("g n -> (g n)").partition_broadcast(P),
-            )
             if (c * LOAD_CODES) % PLANES == 0:
                 load_planes(w2_planes, W2_scales, c * LOAD_CODES // PLANES)
             load_words(w2_words, W2_words, codes)
@@ -99,6 +100,19 @@ def tile_linearwdecoder_pa_e_kernel(tc, z1, z2, W1_words, W1_scales, b1, W2_word
 
         def plane_of(planes, g):
             return planes[4 * (g % PLANES) : P, g // PLANES, :]
+
+        def spread_bias(first):
+            for pair in range(first, first + CODES // LAG_FINISH, 2):
+                bias_bank = banks.tile([P, 2, WIDTH], BF16, tag="bank")
+                for i in range(2):
+                    nc.tensor.matmul(
+                        out=bias_bank[:, i, :],
+                        lhsT=ident_bf16[:, pair + i : pair + i + 1].to_broadcast([P, P]),
+                        rhs=b1_small[:],
+                        start=True,
+                        stop=True,
+                    )
+                nc.vector.tensor_copy(out=b1_rows[:, pair : pair + 2, :], in_=bias_bank[:])
 
         def quantise_z(g):
             z_bank = banks.tile([P, 2, BATCH], F32, tag="bank")
@@ -203,6 +217,8 @@ def tile_linearwdecoder_pa_e_kernel(tc, z1, z2, W1_words, W1_scales, b1, W2_word
             nc.gpsimd.dma_start(out=out.rearrange("(r p) g n -> p r g n", p=P)[:, :, g, :], in_=result[:])
 
         for round_no in range(CODES + LAG_FINISH):
+            if round_no < LAG_FINISH:
+                spread_bias(round_no * (CODES // LAG_FINISH))
             if round_no < CODES:
                 quantise_z(round_no)
             if 0 <= round_no - LAG_HIDDEN < CODES:

@@ -53,15 +53,15 @@ def tile_linearwdecoder_pa_e_kernel(tc, z1, z2, W1_words, W1_scales, b1, W2_word
         b2_cols = resident.tile([P, CODES * COL_TILES], F32)
         ident = resident.tile([P, P], F32)
 
-        nc.vector.memset(w1_planes[:].rearrange("p a n -> p (a n)").bitcast(I32), 0)
-        nc.vector.memset(w2_planes[:].rearrange("p a n -> p (a n)").bitcast(I32), 0)
-        nc.vector.memset(b2_f32[:], 0.0)
         nc.vector.memset(b1_small[:], 0.0)
+        nc.vector.memset(w1_planes[:].rearrange("p a n -> p (a n)").bitcast(I32), 0)
+        nc.vector.memset(b2_f32[:], 0.0)
+        nc.vector.memset(w2_planes[:].rearrange("p a n -> p (a n)").bitcast(I32), 0)
         make_identity(nc, ident_bf16[:])
         make_identity(nc, ident[:])
 
-        nc.sync.dma_start(out=b1_small[0:CODES, :], in_=b1)
         nc.sync.dma_start(out=b2_raw[0 : CODES * COL_TILES, :], in_=b2.rearrange("g (j m) -> (g j) m", m=P))
+        nc.sync.dma_start(out=b1_small[0:CODES, :], in_=b1)
 
         def load_planes(planes, scales, a):
             for quadrant in range(4):
@@ -151,17 +151,17 @@ def tile_linearwdecoder_pa_e_kernel(tc, z1, z2, W1_words, W1_scales, b1, W2_word
                 )
             kept["pre", g] = pre
 
-        def transpose_hidden(g):
+        def transpose_hidden(g, r):
             pre = kept["pre", g]
-            h_grouped = work.tile([P, BATCH, PACK], BF16, align_bytes=64)
-            for r in range(ROW_TILES):
-                h_bank = banks.tile([P, PACK, P], F32, tag="bank")
-                for t in range(PACK):
-                    nc.tensor.transpose(h_bank[:, t, :], pre[:, r, t, :], ident[:])
-                nc.scalar.activation(
-                    out=h_grouped[:, r * P : (r + 1) * P, :], in_=h_bank[:].rearrange("p t b -> p b t"), func=RELU
-                )
-            kept["h_grouped", g] = h_grouped
+            if r == 0:
+                h_grouped = work.tile([P, BATCH, PACK], BF16, align_bytes=64)
+                kept["h_grouped", g] = h_grouped
+            h_bank = banks.tile([P, PACK, P], F32, tag="bank")
+            for t in range(PACK):
+                nc.tensor.transpose(h_bank[:, t, :], pre[:, r, t, :], ident[:])
+            nc.scalar.activation(
+                out=kept["h_grouped", g][:, r * P : (r + 1) * P, :], in_=h_bank[:].rearrange("p t b -> p b t"), func=RELU
+            )
 
         def quantise_hidden(g):
             h_grouped = kept["h_grouped", g]
@@ -217,16 +217,18 @@ def tile_linearwdecoder_pa_e_kernel(tc, z1, z2, W1_words, W1_scales, b1, W2_word
             nc.gpsimd.dma_start(out=out.rearrange("(r p) g n -> p r g n", p=P)[:, :, g, :], in_=result[:])
 
         for round_no in range(CODES + LAG_FINISH):
-            if round_no < LAG_FINISH:
-                spread_bias(round_no * (CODES // LAG_FINISH))
             if round_no < CODES:
                 quantise_z(round_no)
+            if round_no < LAG_FINISH:
+                spread_bias(round_no * (CODES // LAG_FINISH))
             if 0 <= round_no - LAG_HIDDEN < CODES:
-                transpose_hidden(round_no - LAG_HIDDEN)
-            if 0 <= round_no - LAG_FINISH < CODES:
-                finish(round_no - LAG_FINISH)
+                transpose_hidden(round_no - LAG_HIDDEN, 0)
             if 0 <= round_no - LAG_LAYER1 < CODES:
                 layer1(round_no - LAG_LAYER1)
+            if 0 <= round_no - LAG_HIDDEN < CODES:
+                transpose_hidden(round_no - LAG_HIDDEN, 1)
+            if 0 <= round_no - LAG_FINISH < CODES:
+                finish(round_no - LAG_FINISH)
             if 0 <= round_no - LAG_HIDDEN < CODES:
                 quantise_hidden(round_no - LAG_HIDDEN)
             if 0 <= round_no - LAG_LAYER2 < CODES:

@@ -46,7 +46,7 @@ def tile_linearwdecoder_pa_e_kernel(tc, z1, z2, W1_words, W1_scales, b1, W2_word
         w1_planes = resident.tile([P, CODES // PLANES, WIDTH], U8, align_bytes=64)
         w2_planes = resident.tile([P, CODES // PLANES, WIDTH], U8, align_bytes=64)
         b1_small = resident.tile([P, WIDTH], BF16)
-        b1_rows = resident.tile([P, CODES, WIDTH], BF16)
+        b1_sorted = resident.tile([P, CODES, PACK, P], BF16)
         ident_bf16 = resident.tile([P, P], BF16)
         b2_raw = resident.tile([P, P], BF16)
         b2_f32 = resident.tile([P, P], F32)
@@ -112,7 +112,9 @@ def tile_linearwdecoder_pa_e_kernel(tc, z1, z2, W1_words, W1_scales, b1, W2_word
                         start=True,
                         stop=True,
                     )
-                nc.vector.tensor_copy(out=b1_rows[:, pair : pair + 2, :], in_=bias_bank[:])
+                nc.vector.tensor_copy(
+                    out=b1_sorted[:, pair : pair + 2, :, :], in_=bias_bank[:].rearrange("b i (m t) -> b i t m", t=PACK)
+                )
 
         def quantise_z(g):
             z_bank = banks.tile([P, 2, BATCH], F32, tag="bank")
@@ -146,7 +148,7 @@ def tile_linearwdecoder_pa_e_kernel(tc, z1, z2, W1_words, W1_scales, b1, W2_word
                 nc.vector.tensor_tensor(
                     out=pre[:, r, :, :],
                     in0=acc1[:].rearrange("b (m t) -> b t m", t=PACK),
-                    in1=b1_rows[:, g, :].rearrange("b (m t) -> b t m", t=PACK),
+                    in1=b1_sorted[:, g, :, :],
                     op=ADD,
                 )
             kept["pre", g] = pre
@@ -201,7 +203,7 @@ def tile_linearwdecoder_pa_e_kernel(tc, z1, z2, W1_words, W1_scales, b1, W2_word
         def finish(g):
             branch = kept["branch", g]
             pre = kept["pre", g]
-            result = work.tile([P, ROW_TILES, WIDTH], F32, bufs=4)
+            result = work.tile([P, ROW_TILES, WIDTH], F32, bufs=8)
             for r in range(ROW_TILES):
                 back = banks.tile([P, WIDTH], F32, tag="bank")
                 for j in range(COL_TILES):
@@ -214,13 +216,11 @@ def tile_linearwdecoder_pa_e_kernel(tc, z1, z2, W1_words, W1_scales, b1, W2_word
                     op0=MAX,
                     op1=ADD,
                 )
-            nc.gpsimd.dma_start(out=out.rearrange("(r p) g n -> p r g n", p=P)[:, :, g, :], in_=result[:])
+            nc.sync.dma_start(out=out.rearrange("(r p) g n -> p r g n", p=P)[:, :, g, :], in_=result[:])
 
         for round_no in range(CODES + LAG_FINISH):
             if round_no < CODES:
                 quantise_z(round_no)
-            if round_no < LAG_FINISH:
-                spread_bias(round_no * (CODES // LAG_FINISH))
             if 0 <= round_no - LAG_HIDDEN < CODES:
                 transpose_hidden(round_no - LAG_HIDDEN, 0)
             if 0 <= round_no - LAG_LAYER1 < CODES:
@@ -233,3 +233,5 @@ def tile_linearwdecoder_pa_e_kernel(tc, z1, z2, W1_words, W1_scales, b1, W2_word
                 quantise_hidden(round_no - LAG_HIDDEN)
             if 0 <= round_no - LAG_LAYER2 < CODES:
                 layer2(round_no - LAG_LAYER2)
+            if round_no < LAG_FINISH:
+                spread_bias(round_no * (CODES // LAG_FINISH))

@@ -46,6 +46,7 @@ def tile_linearwdecoder_pa_e_kernel(tc, z1, z2, W1_words, W1_scales, b1, W2_word
         w1_planes = resident.tile([P, CODES // PLANES, WIDTH], U8, align_bytes=64)
         w2_planes = resident.tile([P, CODES // PLANES, WIDTH], U8, align_bytes=64)
         b1_small = resident.tile([P, WIDTH], BF16)
+        b1_small_sorted = resident.tile([P, PACK, P], BF16)
         b1_sorted = resident.tile([P, CODES, PACK, P], BF16)
         ident_bf16 = resident.tile([P, P], BF16)
         b2_raw = resident.tile([P, P], BF16)
@@ -90,6 +91,8 @@ def tile_linearwdecoder_pa_e_kernel(tc, z1, z2, W1_words, W1_scales, b1, W2_word
                 load_planes(w2_planes, W2_scales, c * LOAD_CODES // PLANES)
             load_words(w2_words, W2_words, codes)
 
+        nc.vector.tensor_copy(out=b1_small_sorted[:], in_=b1_small[:].rearrange("g (m t) -> g t m", t=PACK))
+
         nc.vector.tensor_copy(out=b2_f32[0 : CODES * COL_TILES, :], in_=b2_raw[0 : CODES * COL_TILES, :])
         b2_bank = banks.tile([P, WIDTH], F32, tag="bank")
         nc.tensor.transpose(b2_bank[:, 0:P], b2_f32[:], ident[:])
@@ -108,12 +111,12 @@ def tile_linearwdecoder_pa_e_kernel(tc, z1, z2, W1_words, W1_scales, b1, W2_word
                     nc.tensor.matmul(
                         out=bias_bank[:, i, :],
                         lhsT=ident_bf16[:, pair + i : pair + i + 1].to_broadcast([P, P]),
-                        rhs=b1_small[:],
+                        rhs=b1_small_sorted[:].rearrange("g t m -> g (t m)"),
                         start=True,
                         stop=True,
                     )
                 nc.vector.tensor_copy(
-                    out=b1_sorted[:, pair : pair + 2, :, :], in_=bias_bank[:].rearrange("b i (m t) -> b i t m", t=PACK)
+                    out=b1_sorted[:, pair : pair + 2, :, :].rearrange("b i t m -> b i (t m)"), in_=bias_bank[:]
                 )
 
         def quantise_z(g):

@@ -19,9 +19,16 @@ BATCH = 256
 ROW_TILES = BATCH // P
 CODES = 16
 HALF = 256
-WIDTH = 512
+WIDTH = 2 * HALF
+PAIRS = WIDTH // 2
 COL_TILES = WIDTH // P
+QUADRANT = 32
+LIVE = 4
 PLANES = 4
+BANK_BYTES = 2048
+WORD_PAIRS = PACK // 2
+BANK_BIASES = BANK_BYTES // (2 * WIDTH)
+BANK_COL_TILES = BANK_BYTES // (4 * BATCH)
 LOAD_CODES = 2
 
 FLOPS = 2 * 2 * BATCH * CODES * WIDTH * WIDTH
@@ -30,14 +37,20 @@ LAG_LAYER1 = 1
 LAG_HIDDEN = 2
 LAG_LAYER2 = 3
 LAG_FINISH = 4
+BIAS_CODES = CODES // LAG_FINISH
+
+STEP_BUFS = 3
+PRE_BUFS = LAG_FINISH - LAG_LAYER1 + 2
+RESULT_BUFS = CODES
+PSUM_BANKS = 8
 
 
 def tile_linearwdecoder_pa_e_kernel(tc, z1, z2, W1_words, W1_scales, b1, W2_words, W2_scales, b2, out):
     nc = tc.nc
     with ExitStack() as stack:
         resident = stack.enter_context(tc.tile_pool(name="resident", bufs=1))
-        work = stack.enter_context(tc.tile_pool(name="work", bufs=3))
-        banks = stack.enter_context(tc.psum_pool(name="banks", bufs=8))
+        work = stack.enter_context(tc.tile_pool(name="work", bufs=STEP_BUFS))
+        banks = stack.enter_context(tc.psum_pool(name="banks", bufs=PSUM_BANKS))
         stack.enter_context(tc.manual_schedule())
 
         z_rows = resident.tile([P, ROW_TILES, CODES, WIDTH], BF16)
@@ -45,196 +58,196 @@ def tile_linearwdecoder_pa_e_kernel(tc, z1, z2, W1_words, W1_scales, b1, W2_word
         w2_words = resident.tile([P, CODES, WIDTH], U32, align_bytes=64)
         w1_planes = resident.tile([P, CODES // PLANES, WIDTH], U8, align_bytes=64)
         w2_planes = resident.tile([P, CODES // PLANES, WIDTH], U8, align_bytes=64)
-        b1_small = resident.tile([P, WIDTH], BF16)
-        b1_small_sorted = resident.tile([P, PACK, P], BF16)
-        b1_sorted = resident.tile([P, CODES, PACK, P], BF16)
+        b1_by_code = resident.tile([P, WIDTH], BF16)
+        b1_by_code_sorted = resident.tile([P, PACK, P], BF16)
+        b1_spread = resident.tile([P, CODES, PACK, P], BF16)
+        b2_by_tile = resident.tile([P, P], BF16)
+        b2_columns = resident.tile([P, CODES * COL_TILES], F32)
+        ident_f32 = resident.tile([P, P], F32)
         ident_bf16 = resident.tile([P, P], BF16)
-        b2_raw = resident.tile([P, P], BF16)
-        b2_f32 = resident.tile([P, P], F32)
-        b2_cols = resident.tile([P, CODES * COL_TILES], F32)
-        ident = resident.tile([P, P], F32)
 
-        nc.vector.memset(b1_small[:], 0.0)
+        nc.vector.memset(b2_by_tile[:], 0.0)
+        nc.vector.memset(b1_by_code[:], 0.0)
         nc.vector.memset(w1_planes[:].rearrange("p a n -> p (a n)").bitcast(I32), 0)
-        nc.vector.memset(b2_f32[:], 0.0)
         nc.vector.memset(w2_planes[:].rearrange("p a n -> p (a n)").bitcast(I32), 0)
         make_identity(nc, ident_bf16[:])
-        make_identity(nc, ident[:])
+        make_identity(nc, ident_f32[:])
 
-        nc.sync.dma_start(out=b2_raw[0 : CODES * COL_TILES, :], in_=b2.rearrange("g (j m) -> (g j) m", m=P))
-        nc.sync.dma_start(out=b1_small[0:CODES, :], in_=b1)
 
-        def load_planes(planes, scales, a):
-            for quadrant in range(4):
+        def load_planes(planes, scales, group):
+            for quadrant in range(P // QUADRANT):
                 nc.sync.dma_start(
-                    out=planes[32 * quadrant : 32 * quadrant + 4 * PLANES, a, :].bitcast(I32),
-                    in_=scales[PLANES * a : PLANES * (a + 1), 4 * quadrant : 4 * quadrant + 4, :].bitcast(I32),
+                    out=planes[QUADRANT * quadrant : QUADRANT * quadrant + LIVE * PLANES, group, :].bitcast(I32),
+                    in_=scales[PLANES * group : PLANES * (group + 1), LIVE * quadrant : LIVE * (quadrant + 1), :].bitcast(I32),
                 )
 
         def load_words(words, packed, codes):
             nc.sync.dma_start(
-                out=words[:, codes, :].bitcast(I32),
-                in_=packed[codes].rearrange("g p n t -> p g (n t)").bitcast(I32),
+                out=words[:, codes, :].bitcast(I32), in_=packed[codes].rearrange("g p n t -> p g (n t)").bitcast(I32)
             )
 
-        for c in range(CODES // LOAD_CODES):
-            codes = slice(c * LOAD_CODES, (c + 1) * LOAD_CODES)
-            cols = slice(c * LOAD_CODES * HALF, (c + 1) * LOAD_CODES * HALF)
+        nc.sync.dma_start(out=b2_by_tile[0 : CODES * COL_TILES, :], in_=b2.rearrange("g (j m) -> (g j) m", m=P))
+        nc.sync.dma_start(out=b1_by_code[0:CODES, :], in_=b1)
+        for first in range(0, CODES, LOAD_CODES):
+            codes = slice(first, first + LOAD_CODES)
+            z_cols = slice(first * HALF, (first + LOAD_CODES) * HALF)
             for r in range(ROW_TILES):
                 rows = slice(r * P, (r + 1) * P)
-                nc.sync.dma_start(out=z_rows[:, r, codes, 0:HALF], in_=z1[rows, cols].rearrange("p (g k) -> p g k", k=HALF))
-                nc.sync.dma_start(out=z_rows[:, r, codes, HALF:WIDTH], in_=z2[rows, cols].rearrange("p (g k) -> p g k", k=HALF))
-            if (c * LOAD_CODES) % PLANES == 0:
-                load_planes(w1_planes, W1_scales, c * LOAD_CODES // PLANES)
+                nc.sync.dma_start(out=z_rows[:, r, codes, 0:HALF], in_=z1[rows, z_cols].rearrange("b (g k) -> b g k", k=HALF))
+                nc.sync.dma_start(out=z_rows[:, r, codes, HALF:WIDTH], in_=z2[rows, z_cols].rearrange("b (g k) -> b g k", k=HALF))
+            if first % PLANES == 0:
+                load_planes(w1_planes, W1_scales, first // PLANES)
             load_words(w1_words, W1_words, codes)
-            if (c * LOAD_CODES) % PLANES == 0:
-                load_planes(w2_planes, W2_scales, c * LOAD_CODES // PLANES)
+            if first % PLANES == 0:
+                load_planes(w2_planes, W2_scales, first // PLANES)
             load_words(w2_words, W2_words, codes)
 
-        nc.vector.tensor_copy(out=b1_small_sorted[:], in_=b1_small[:].rearrange("g (m t) -> g t m", t=PACK))
-
-        nc.vector.tensor_copy(out=b2_f32[0 : CODES * COL_TILES, :], in_=b2_raw[0 : CODES * COL_TILES, :])
-        b2_bank = banks.tile([P, WIDTH], F32, tag="bank")
-        nc.tensor.transpose(b2_bank[:, 0:P], b2_f32[:], ident[:])
-        nc.vector.tensor_copy(out=b2_cols[:], in_=b2_bank[:, 0 : CODES * COL_TILES])
-
-        z_words = z_rows[:].bitcast(F32)
-        kept = {}
-
         def plane_of(planes, g):
-            return planes[4 * (g % PLANES) : P, g // PLANES, :]
+            return planes[LIVE * (g % PLANES) : P, g // PLANES, :]
+
+
+        b2_bank = banks.tile([P, BANK_BYTES // 2], BF16, tag="bank")
+        nc.tensor.transpose(b2_bank[:, 0:P], b2_by_tile[:], ident_bf16[:])
+        nc.vector.tensor_copy(out=b2_columns[:], in_=b2_bank[:, 0 : CODES * COL_TILES])
+
+        nc.vector.tensor_copy(out=b1_by_code_sorted[:], in_=b1_by_code[:].rearrange("g (m t) -> g t m", t=PACK))
 
         def spread_bias(first):
-            for pair in range(first, first + CODES // LAG_FINISH, 2):
-                bias_bank = banks.tile([P, 2, WIDTH], BF16, tag="bank")
-                for i in range(2):
+            for g in range(first, first + BIAS_CODES, BANK_BIASES):
+                bias_bank = banks.tile([P, BANK_BIASES, WIDTH], BF16, tag="bank")
+                for i in range(BANK_BIASES):
                     nc.tensor.matmul(
                         out=bias_bank[:, i, :],
-                        lhsT=ident_bf16[:, pair + i : pair + i + 1].to_broadcast([P, P]),
-                        rhs=b1_small_sorted[:].rearrange("g t m -> g (t m)"),
+                        lhsT=ident_bf16[:, g + i : g + i + 1].to_broadcast([P, P]),
+                        rhs=b1_by_code_sorted[:].rearrange("g t m -> g (t m)"),
                         start=True,
                         stop=True,
                     )
                 nc.vector.tensor_copy(
-                    out=b1_sorted[:, pair : pair + 2, :, :].rearrange("b i t m -> b i (t m)"), in_=bias_bank[:]
+                    out=b1_spread[:, g : g + BANK_BIASES, :, :].rearrange("b i t m -> b i (t m)"), in_=bias_bank[:]
                 )
 
+        z_pairs = z_rows[:].bitcast(F32)
+        z_quantised = {}
+        pre_of = {}
+        h_grouped_of = {}
+        h_quantised = {}
+        branch_of = {}
+
         def quantise_z(g):
-            z_bank = banks.tile([P, 2, BATCH], F32, tag="bank")
+            z_bank = banks.tile([P, WORD_PAIRS, BATCH], F32, tag="bank")
             for r in range(ROW_TILES):
-                for u in range(2):
-                    nc.tensor.transpose(z_bank[:, u, r * P : (r + 1) * P], z_words[:, r, g, u : HALF : 2], ident[:])
+                for u in range(WORD_PAIRS):
+                    nc.tensor.transpose(
+                        z_bank[:, u, r * P : (r + 1) * P], z_pairs[:, r, g, u:PAIRS:WORD_PAIRS], ident_f32[:]
+                    )
             z_grouped = work.tile([P, BATCH, PACK], BF16, align_bytes=64)
             nc.scalar.copy(out=z_grouped[:].bitcast(F32), in_=z_bank[:].rearrange("p u b -> p b u"))
-            z_codes = work.tile([P, BATCH], U32, align_bytes=64)
-            z_scales = work.tile([P, BATCH], U8, align_bytes=64)
+            z_words = work.tile([P, BATCH], U32, align_bytes=64)
+            z_plane = work.tile([P, BATCH], U8, align_bytes=64)
             nc.vector.quantize_mx(
-                out=z_codes[:].bitcast(FP8X4), scales=z_scales[:], in_=z_grouped[:].rearrange("p b t -> p (b t)")
+                out=z_words[:].bitcast(FP8X4), scales=z_plane[:], in_=z_grouped[:].rearrange("p b t -> p (b t)")
             )
-            kept["z", g] = (z_codes, z_scales)
+            z_quantised[g] = (z_words, z_plane)
 
         def layer1(g):
-            z_codes, z_scales = kept["z", g]
-            pre = work.tile([P, ROW_TILES, PACK, P], F32, bufs=6)
+            z_words, z_plane = z_quantised[g]
+            pre = work.tile([P, ROW_TILES, PACK, P], F32, bufs=PRE_BUFS)
             for r in range(ROW_TILES):
                 rows = slice(r * P, (r + 1) * P)
                 acc1 = banks.tile([P, WIDTH], F32, tag="bank")
                 nc.tensor.matmul_mx(
                     out=acc1[:],
-                    lhsT=z_codes[:, rows].bitcast(FP8X4),
-                    lhsT_scale=z_scales[:, rows],
+                    lhsT=z_words[:, rows].bitcast(FP8X4),
+                    lhsT_scale=z_plane[:, rows],
                     rhs=w1_words[:, g, :].bitcast(FP8X4),
                     rhs_scale=plane_of(w1_planes, g),
                     start=True,
                     stop=True,
                 )
                 nc.vector.tensor_tensor(
-                    out=pre[:, r, :, :],
-                    in0=acc1[:].rearrange("b (m t) -> b t m", t=PACK),
-                    in1=b1_sorted[:, g, :, :],
-                    op=ADD,
+                    out=pre[:, r, :, :], in0=acc1[:].rearrange("b (m t) -> b t m", t=PACK), in1=b1_spread[:, g, :, :], op=ADD
                 )
-            kept["pre", g] = pre
+            pre_of[g] = pre
 
-        def transpose_hidden(g, r):
-            pre = kept["pre", g]
-            if r == 0:
-                h_grouped = work.tile([P, BATCH, PACK], BF16, align_bytes=64)
-                kept["h_grouped", g] = h_grouped
-            h_bank = banks.tile([P, PACK, P], F32, tag="bank")
-            for t in range(PACK):
-                nc.tensor.transpose(h_bank[:, t, :], pre[:, r, t, :], ident[:])
-            nc.scalar.activation(
-                out=kept["h_grouped", g][:, r * P : (r + 1) * P, :], in_=h_bank[:].rearrange("p t b -> p b t"), func=RELU
-            )
+        def transpose_hidden(g):
+            h_grouped = work.tile([P, BATCH, PACK], BF16, align_bytes=64)
+            for r in range(ROW_TILES):
+                h_bank = banks.tile([P, PACK, P], F32, tag="bank")
+                for t in range(PACK):
+                    nc.tensor.transpose(h_bank[:, t, :], pre_of[g][:, r, t, :], ident_f32[:])
+                nc.scalar.activation(
+                    out=h_grouped[:, r * P : (r + 1) * P, :], in_=h_bank[:].rearrange("p t b -> p b t"), func=RELU
+                )
+            h_grouped_of[g] = h_grouped
 
         def quantise_hidden(g):
-            h_grouped = kept["h_grouped", g]
-            h_codes = work.tile([P, BATCH], U32, align_bytes=64)
-            h_scales = work.tile([P, BATCH], U8, align_bytes=64)
+            h_words = work.tile([P, BATCH], U32, align_bytes=64)
+            h_plane = work.tile([P, BATCH], U8, align_bytes=64)
             nc.vector.quantize_mx(
-                out=h_codes[:].bitcast(FP8X4), scales=h_scales[:], in_=h_grouped[:].rearrange("p b t -> p (b t)")
+                out=h_words[:].bitcast(FP8X4), scales=h_plane[:], in_=h_grouped_of[g][:].rearrange("p b t -> p (b t)")
             )
-            kept["h", g] = (h_codes, h_scales)
+            h_quantised[g] = (h_words, h_plane)
 
         def layer2(g):
-            h_codes, h_scales = kept["h", g]
+            h_words, h_plane = h_quantised[g]
             branch = work.tile([P, COL_TILES, BATCH], F32)
-            for half in range(COL_TILES // 2):
-                acc2 = banks.tile([P, 2, BATCH], F32, tag="bank")
-                for i in range(2):
-                    j = 2 * half + i
+            for bank_no in range(COL_TILES // BANK_COL_TILES):
+                acc2 = banks.tile([P, BANK_COL_TILES, BATCH], F32, tag="bank")
+                for i in range(BANK_COL_TILES):
+                    j = BANK_COL_TILES * bank_no + i
                     nc.tensor.matmul_mx(
                         out=acc2[:, i, :],
                         lhsT=w2_words[:, g, j * P : (j + 1) * P].bitcast(FP8X4),
                         lhsT_scale=plane_of(w2_planes, g)[:, j * P : (j + 1) * P],
-                        rhs=h_codes[:].bitcast(FP8X4),
-                        rhs_scale=h_scales[:],
+                        rhs=h_words[:].bitcast(FP8X4),
+                        rhs_scale=h_plane[:],
                         start=True,
                         stop=True,
                     )
-                for i in range(2):
-                    j = 2 * half + i
+                for i in range(BANK_COL_TILES):
+                    j = BANK_COL_TILES * bank_no + i
                     nc.scalar.activation(
                         out=branch[:, j, :],
                         in_=acc2[:, i, :],
                         func=RELU,
-                        bias=b2_cols[:, COL_TILES * g + j : COL_TILES * g + j + 1],
+                        bias=b2_columns[:, COL_TILES * g + j : COL_TILES * g + j + 1],
                     )
-            kept["branch", g] = branch
+            branch_of[g] = branch
 
         def finish(g):
-            branch = kept["branch", g]
-            pre = kept["pre", g]
-            result = work.tile([P, ROW_TILES, WIDTH], F32, bufs=8)
             for r in range(ROW_TILES):
+                rows = slice(r * P, (r + 1) * P)
                 back = banks.tile([P, WIDTH], F32, tag="bank")
                 for j in range(COL_TILES):
-                    nc.tensor.transpose(back[:, j * P : (j + 1) * P], branch[:, j, r * P : (r + 1) * P], ident[:])
+                    nc.tensor.transpose(back[:, j * P : (j + 1) * P], branch_of[g][:, j, rows], ident_f32[:])
+                result = work.tile([P, WIDTH], F32, bufs=RESULT_BUFS)
                 nc.vector.scalar_tensor_tensor(
-                    out=result[:, r, :].rearrange("b (m t) -> b m t", t=PACK),
-                    in0=pre[:, r, :, :].rearrange("b t m -> b m t"),
+                    out=result[:].rearrange("b (m t) -> b m t", t=PACK),
+                    in0=pre_of[g][:, r, :, :].rearrange("b t m -> b m t"),
                     scalar=0.0,
                     in1=back[:].rearrange("b (m t) -> b m t", t=PACK),
                     op0=MAX,
                     op1=ADD,
                 )
-            nc.sync.dma_start(out=out.rearrange("(r p) g n -> p r g n", p=P)[:, :, g, :], in_=result[:])
+                nc.sync.dma_start(out=out[rows, g, :], in_=result[:])
+
+
+        def in_flight(g):
+            return 0 <= g < CODES
 
         for round_no in range(CODES + LAG_FINISH):
-            if round_no < CODES:
+            if in_flight(round_no):
                 quantise_z(round_no)
-            if 0 <= round_no - LAG_HIDDEN < CODES:
-                transpose_hidden(round_no - LAG_HIDDEN, 0)
-            if 0 <= round_no - LAG_LAYER1 < CODES:
+            if in_flight(round_no - LAG_HIDDEN):
+                transpose_hidden(round_no - LAG_HIDDEN)
+            if in_flight(round_no - LAG_LAYER1):
                 layer1(round_no - LAG_LAYER1)
-            if 0 <= round_no - LAG_HIDDEN < CODES:
-                transpose_hidden(round_no - LAG_HIDDEN, 1)
-            if 0 <= round_no - LAG_FINISH < CODES:
+            if in_flight(round_no - LAG_FINISH):
                 finish(round_no - LAG_FINISH)
-            if 0 <= round_no - LAG_HIDDEN < CODES:
+            if in_flight(round_no - LAG_HIDDEN):
                 quantise_hidden(round_no - LAG_HIDDEN)
-            if 0 <= round_no - LAG_LAYER2 < CODES:
+            if in_flight(round_no - LAG_LAYER2):
                 layer2(round_no - LAG_LAYER2)
             if round_no < LAG_FINISH:
-                spread_bias(round_no * (CODES // LAG_FINISH))
+                spread_bias(round_no * BIAS_CODES)

@@ -26,7 +26,8 @@ QUADRANT = 32
 LIVE = 4
 PLANES = 4
 BANK_BYTES = 2048
-WORD_PAIRS = PACK // 2
+PAIR = 2
+WORD_PAIRS = PACK // PAIR
 BANK_BIASES = BANK_BYTES // (2 * WIDTH)
 BANK_COL_TILES = BANK_BYTES // (4 * BATCH)
 LOAD_CODES = 2
@@ -59,8 +60,7 @@ def tile_linearwdecoder_pa_e_kernel(tc, z1, z2, W1_words, W1_scales, b1, W2_word
         w1_planes = resident.tile([P, CODES // PLANES, WIDTH], U8, align_bytes=64)
         w2_planes = resident.tile([P, CODES // PLANES, WIDTH], U8, align_bytes=64)
         b1_by_code = resident.tile([P, WIDTH], BF16)
-        b1_by_code_sorted = resident.tile([P, PACK, P], BF16)
-        b1_spread = resident.tile([P, CODES, PACK, P], BF16)
+        b1_spread = resident.tile([P, CODES, WIDTH], BF16)
         b2_by_tile = resident.tile([P, P], BF16)
         b2_columns = resident.tile([P, CODES * COL_TILES], F32)
         ident_f32 = resident.tile([P, P], F32)
@@ -110,8 +110,6 @@ def tile_linearwdecoder_pa_e_kernel(tc, z1, z2, W1_words, W1_scales, b1, W2_word
         nc.tensor.transpose(b2_bank[:, 0:P], b2_by_tile[:], ident_bf16[:])
         nc.vector.tensor_copy(out=b2_columns[:], in_=b2_bank[:, 0 : CODES * COL_TILES])
 
-        nc.vector.tensor_copy(out=b1_by_code_sorted[:], in_=b1_by_code[:].rearrange("g (m t) -> g t m", t=PACK))
-
         def spread_bias(first):
             for g in range(first, first + BIAS_CODES, BANK_BIASES):
                 bias_bank = banks.tile([P, BANK_BIASES, WIDTH], BF16, tag="bank")
@@ -119,17 +117,16 @@ def tile_linearwdecoder_pa_e_kernel(tc, z1, z2, W1_words, W1_scales, b1, W2_word
                     nc.tensor.matmul(
                         out=bias_bank[:, i, :],
                         lhsT=ident_bf16[:, g + i : g + i + 1].to_broadcast([P, P]),
-                        rhs=b1_by_code_sorted[:].rearrange("g t m -> g (t m)"),
+                        rhs=b1_by_code[:],
                         start=True,
                         stop=True,
                     )
-                nc.vector.tensor_copy(
-                    out=b1_spread[:, g : g + BANK_BIASES, :, :].rearrange("b i t m -> b i (t m)"), in_=bias_bank[:]
-                )
+                nc.vector.tensor_copy(out=b1_spread[:, g : g + BANK_BIASES, :], in_=bias_bank[:])
 
         z_pairs = z_rows[:].bitcast(F32)
         z_quantised = {}
         pre_of = {}
+        h_rows_of = {}
         h_grouped_of = {}
         h_quantised = {}
         branch_of = {}
@@ -152,7 +149,8 @@ def tile_linearwdecoder_pa_e_kernel(tc, z1, z2, W1_words, W1_scales, b1, W2_word
 
         def layer1(g):
             z_words, z_plane = z_quantised[g]
-            pre = work.tile([P, ROW_TILES, PACK, P], F32, bufs=PRE_BUFS)
+            pre = work.tile([P, ROW_TILES, WIDTH], F32, bufs=PRE_BUFS)
+            h_rows = work.tile([P, ROW_TILES, WORD_PAIRS, P, PAIR], BF16)
             for r in range(ROW_TILES):
                 rows = slice(r * P, (r + 1) * P)
                 acc1 = banks.tile([P, WIDTH], F32, tag="bank")
@@ -165,20 +163,29 @@ def tile_linearwdecoder_pa_e_kernel(tc, z1, z2, W1_words, W1_scales, b1, W2_word
                     start=True,
                     stop=True,
                 )
-                nc.vector.tensor_tensor(
-                    out=pre[:, r, :, :], in0=acc1[:].rearrange("b (m t) -> b t m", t=PACK), in1=b1_spread[:, g, :, :], op=ADD
+                nc.vector.tensor_tensor(out=pre[:, r, :], in0=acc1[:], in1=b1_spread[:, g, :], op=ADD)
+                nc.gpsimd.tensor_scalar(
+                    out=h_rows[:, r, :, :, :],
+                    in0=pre[:, r, :].rearrange("b (m u e) -> b u m e", u=WORD_PAIRS, e=PAIR),
+                    scalar1=0.0,
+                    scalar2=0.0,
+                    op0=MAX,
+                    op1=ADD,
                 )
             pre_of[g] = pre
+            h_rows_of[g] = h_rows
 
         def transpose_hidden(g):
             h_grouped = work.tile([P, BATCH, PACK], BF16, align_bytes=64)
+            h_bank = banks.tile([P, WORD_PAIRS, BATCH], F32, tag="bank")
             for r in range(ROW_TILES):
-                h_bank = banks.tile([P, PACK, P], F32, tag="bank")
-                for t in range(PACK):
-                    nc.tensor.transpose(h_bank[:, t, :], pre_of[g][:, r, t, :], ident_f32[:])
-                nc.scalar.activation(
-                    out=h_grouped[:, r * P : (r + 1) * P, :], in_=h_bank[:].rearrange("p t b -> p b t"), func=RELU
-                )
+                for u in range(WORD_PAIRS):
+                    nc.tensor.transpose(
+                        h_bank[:, u, r * P : (r + 1) * P],
+                        h_rows_of[g][:, r, u, :, :].rearrange("b m e -> b (m e)").bitcast(F32),
+                        ident_f32[:],
+                    )
+            nc.scalar.copy(out=h_grouped[:].bitcast(F32), in_=h_bank[:].rearrange("p u b -> p b u"))
             h_grouped_of[g] = h_grouped
 
         def quantise_hidden(g):
@@ -223,10 +230,10 @@ def tile_linearwdecoder_pa_e_kernel(tc, z1, z2, W1_words, W1_scales, b1, W2_word
                     nc.tensor.transpose(back[:, j * P : (j + 1) * P], branch_of[g][:, j, rows], ident_f32[:])
                 result = work.tile([P, WIDTH], F32, bufs=RESULT_BUFS)
                 nc.vector.scalar_tensor_tensor(
-                    out=result[:].rearrange("b (m t) -> b m t", t=PACK),
-                    in0=pre_of[g][:, r, :, :].rearrange("b t m -> b m t"),
+                    out=result[:],
+                    in0=pre_of[g][:, r, :],
                     scalar=0.0,
-                    in1=back[:].rearrange("b (m t) -> b m t", t=PACK),
+                    in1=back[:],
                     op0=MAX,
                     op1=ADD,
                 )

@@ -12,6 +12,7 @@ FP8X4 = mybir.dt.float8_e4m3fn_x4
 RELU = mybir.ActivationFunctionType.Relu
 ADD = mybir.AluOpType.add
 MAX = mybir.AluOpType.max
+MULT = mybir.AluOpType.mult
 
 P = 128
 PACK = 4
@@ -35,10 +36,11 @@ LOAD_CODES = 2
 FLOPS = 2 * 2 * BATCH * CODES * WIDTH * WIDTH
 
 LAG_LAYER1 = 1
-LAG_HIDDEN = 2
-LAG_LAYER2 = 3
-LAG_FINISH = 4
-BIAS_CODES = CODES // LAG_FINISH
+LAG_HIDDEN = 3
+LAG_LAYER2 = 4
+LAG_FINISH = 5
+BIAS_ROUNDS = 4
+BIAS_CODES = CODES // BIAS_ROUNDS
 
 STEP_BUFS = 3
 PRE_BUFS = LAG_FINISH - LAG_LAYER1 + 2
@@ -167,9 +169,9 @@ def tile_linearwdecoder_pa_e_kernel(tc, z1, z2, W1_words, W1_scales, b1, W2_word
                 nc.gpsimd.tensor_scalar(
                     out=h_rows[:, r, :, :, :],
                     in0=pre[:, r, :].rearrange("b (m u e) -> b u m e", u=WORD_PAIRS, e=PAIR),
-                    scalar1=0.0,
+                    scalar1=1.0,
                     scalar2=0.0,
-                    op0=MAX,
+                    op0=MULT,
                     op1=ADD,
                 )
             pre_of[g] = pre
@@ -185,7 +187,11 @@ def tile_linearwdecoder_pa_e_kernel(tc, z1, z2, W1_words, W1_scales, b1, W2_word
                         h_rows_of[g][:, r, u, :, :].rearrange("b m e -> b (m e)").bitcast(F32),
                         ident_f32[:],
                     )
-            nc.scalar.copy(out=h_grouped[:].bitcast(F32), in_=h_bank[:].rearrange("p u b -> p b u"))
+            nc.scalar.activation(
+                out=h_grouped[:].rearrange("p b (u e) -> p b u e", u=WORD_PAIRS),
+                in_=h_bank[:].rearrange("p u b -> p (u b)").bitcast(BF16).rearrange("p (u b e) -> p b u e", u=WORD_PAIRS, e=PAIR),
+                func=RELU,
+            )
             h_grouped_of[g] = h_grouped
 
         def quantise_hidden(g):
@@ -256,5 +262,5 @@ def tile_linearwdecoder_pa_e_kernel(tc, z1, z2, W1_words, W1_scales, b1, W2_word
                 quantise_hidden(round_no - LAG_HIDDEN)
             if in_flight(round_no - LAG_LAYER2):
                 layer2(round_no - LAG_LAYER2)
-            if round_no < LAG_FINISH:
+            if round_no < BIAS_ROUNDS:
                 spread_bias(round_no * BIAS_CODES)

@@ -31,21 +31,16 @@ PAIR = 2
 WORD_PAIRS = PACK // PAIR
 BANK_BIASES = BANK_BYTES // (2 * WIDTH)
 BANK_COL_TILES = BANK_BYTES // (4 * BATCH)
-LOAD_CODES = 2
 
 FLOPS = 2 * 2 * BATCH * CODES * WIDTH * WIDTH
 
-LAG_LAYER1 = 1
-LAG_HIDDEN = 3
-LAG_LAYER2 = 4
-LAG_FINISH = 5
-BIAS_ROUNDS = 4
-BIAS_CODES = CODES // BIAS_ROUNDS
-
-STEP_BUFS = 3
-PRE_BUFS = LAG_FINISH - LAG_LAYER1 + 2
-RESULT_BUFS = CODES
+STEP_BUFS = 4
+PRE_BUFS = 8
+RESULT_BUFS = 16
 PSUM_BANKS = 8
+LOAD_CODES = 2
+W2_LAG = 4
+ROUNDS = CODES + 7
 
 
 def tile_linearwdecoder_pa_e_kernel(tc, z1, z2, W1_words, W1_scales, b1, W2_words, W2_scales, b2, out):
@@ -68,9 +63,9 @@ def tile_linearwdecoder_pa_e_kernel(tc, z1, z2, W1_words, W1_scales, b1, W2_word
         ident_f32 = resident.tile([P, P], F32)
         ident_bf16 = resident.tile([P, P], BF16)
 
-        nc.vector.memset(b2_by_tile[:], 0.0)
         nc.vector.memset(b1_by_code[:], 0.0)
         nc.vector.memset(w1_planes[:].rearrange("p a n -> p (a n)").bitcast(I32), 0)
+        nc.vector.memset(b2_by_tile[:], 0.0)
         nc.vector.memset(w2_planes[:].rearrange("p a n -> p (a n)").bitcast(I32), 0)
         make_identity(nc, ident_bf16[:])
         make_identity(nc, ident_f32[:])
@@ -83,76 +78,104 @@ def tile_linearwdecoder_pa_e_kernel(tc, z1, z2, W1_words, W1_scales, b1, W2_word
                     in_=scales[PLANES * group : PLANES * (group + 1), LIVE * quadrant : LIVE * (quadrant + 1), :].bitcast(I32),
                 )
 
-        def load_words(words, packed, codes):
+        def load_words(words, packed, first, count):
+            codes = slice(first, first + count)
             nc.sync.dma_start(
                 out=words[:, codes, :].bitcast(I32), in_=packed[codes].rearrange("g p n t -> p g (n t)").bitcast(I32)
             )
 
-        nc.sync.dma_start(out=b2_by_tile[0 : CODES * COL_TILES, :], in_=b2.rearrange("g (j m) -> (g j) m", m=P))
-        nc.sync.dma_start(out=b1_by_code[0:CODES, :], in_=b1)
-        for first in range(0, CODES, LOAD_CODES):
-            codes = slice(first, first + LOAD_CODES)
-            z_cols = slice(first * HALF, (first + LOAD_CODES) * HALF)
+        def load_z(first, count):
+            codes = slice(first, first + count)
+            z_cols = slice(first * HALF, (first + count) * HALF)
             for r in range(ROW_TILES):
                 rows = slice(r * P, (r + 1) * P)
-                nc.sync.dma_start(out=z_rows[:, r, codes, 0:HALF], in_=z1[rows, z_cols].rearrange("b (g k) -> b g k", k=HALF))
-                nc.sync.dma_start(out=z_rows[:, r, codes, HALF:WIDTH], in_=z2[rows, z_cols].rearrange("b (g k) -> b g k", k=HALF))
-            if first % PLANES == 0:
-                load_planes(w1_planes, W1_scales, first // PLANES)
-            load_words(w1_words, W1_words, codes)
-            if first % PLANES == 0:
-                load_planes(w2_planes, W2_scales, first // PLANES)
-            load_words(w2_words, W2_words, codes)
+                for half, z in enumerate((z1, z2)):
+                    nc.sync.dma_start(
+                        out=z_rows[:, r, codes, half * HALF : (half + 1) * HALF],
+                        in_=z[rows, z_cols].rearrange("b (g k) -> b g k", k=HALF),
+                    )
+
+        def load_b1():
+            nc.sync.dma_start(out=b1_by_code[0:CODES, :], in_=b1)
+
+        def load_b2():
+            nc.sync.dma_start(out=b2_by_tile[0 : CODES * COL_TILES, :], in_=b2.rearrange("g (j m) -> (g j) m", m=P))
+
+        load_b1()
+        for first in range(0, CODES + W2_LAG, LOAD_CODES):
+            if first < CODES:
+                load_z(first, LOAD_CODES)
+                if first % PLANES == 0:
+                    load_planes(w1_planes, W1_scales, first // PLANES)
+                load_words(w1_words, W1_words, first, LOAD_CODES)
+            if first == 0:
+                load_b2()
+            late = first - W2_LAG
+            if late >= 0:
+                if late % PLANES == 0:
+                    load_planes(w2_planes, W2_scales, late // PLANES)
+                load_words(w2_words, W2_words, late, LOAD_CODES)
 
         def plane_of(planes, g):
             return planes[LIVE * (g % PLANES) : P, g // PLANES, :]
 
 
-        b2_bank = banks.tile([P, BANK_BYTES // 2], BF16, tag="bank")
-        nc.tensor.transpose(b2_bank[:, 0:P], b2_by_tile[:], ident_bf16[:])
-        nc.vector.tensor_copy(out=b2_columns[:], in_=b2_bank[:, 0 : CODES * COL_TILES])
+        def columns_of_b2():
+            b2_bank = banks.tile([P, BANK_BYTES // 2], BF16, tag="bank")
+            nc.tensor.transpose(b2_bank[:, 0:P], b2_by_tile[:], ident_bf16[:])
+            nc.vector.tensor_copy(out=b2_columns[:], in_=b2_bank[:, 0 : CODES * COL_TILES])
 
         def spread_bias(first):
-            for g in range(first, first + BIAS_CODES, BANK_BIASES):
-                bias_bank = banks.tile([P, BANK_BIASES, WIDTH], BF16, tag="bank")
-                for i in range(BANK_BIASES):
-                    nc.tensor.matmul(
-                        out=bias_bank[:, i, :],
-                        lhsT=ident_bf16[:, g + i : g + i + 1].to_broadcast([P, P]),
-                        rhs=b1_by_code[:],
-                        start=True,
-                        stop=True,
-                    )
-                nc.vector.tensor_copy(out=b1_spread[:, g : g + BANK_BIASES, :], in_=bias_bank[:])
+            bias_bank = banks.tile([P, BANK_BIASES, WIDTH], BF16, tag="bank")
+            for i in range(BANK_BIASES):
+                nc.tensor.matmul(
+                    out=bias_bank[:, i, :],
+                    lhsT=ident_bf16[:, first + i : first + i + 1].to_broadcast([P, P]),
+                    rhs=b1_by_code[:],
+                    start=True,
+                    stop=True,
+                )
+            nc.scalar.copy(out=b1_spread[:, first : first + BANK_BIASES, :], in_=bias_bank[:])
 
         z_pairs = z_rows[:].bitcast(F32)
+        z_bank_of = {}
+        z_grouped_of = {}
         z_quantised = {}
+        acc1_of = {}
         pre_of = {}
         h_rows_of = {}
+        h_bank_of = {}
         h_grouped_of = {}
         h_quantised = {}
+        acc2_of = {}
         branch_of = {}
+        back_of = {}
 
-        def quantise_z(g):
+        def transpose_z(g):
             z_bank = banks.tile([P, WORD_PAIRS, BATCH], F32, tag="bank")
             for r in range(ROW_TILES):
                 for u in range(WORD_PAIRS):
                     nc.tensor.transpose(
                         z_bank[:, u, r * P : (r + 1) * P], z_pairs[:, r, g, u:PAIRS:WORD_PAIRS], ident_f32[:]
                     )
+            z_bank_of[g] = z_bank
+
+        def copy_z(g):
             z_grouped = work.tile([P, BATCH, PACK], BF16, align_bytes=64)
-            nc.scalar.copy(out=z_grouped[:].bitcast(F32), in_=z_bank[:].rearrange("p u b -> p b u"))
+            nc.scalar.copy(out=z_grouped[:].bitcast(F32), in_=z_bank_of[g][:].rearrange("p u b -> p b u"))
+            z_grouped_of[g] = z_grouped
+
+        def quantise_z(g):
             z_words = work.tile([P, BATCH], U32, align_bytes=64)
             z_plane = work.tile([P, BATCH], U8, align_bytes=64)
             nc.vector.quantize_mx(
-                out=z_words[:].bitcast(FP8X4), scales=z_plane[:], in_=z_grouped[:].rearrange("p b t -> p (b t)")
+                out=z_words[:].bitcast(FP8X4), scales=z_plane[:], in_=z_grouped_of[g][:].rearrange("p b t -> p (b t)")
             )
             z_quantised[g] = (z_words, z_plane)
 
-        def layer1(g):
+        def multiply1(g):
             z_words, z_plane = z_quantised[g]
-            pre = work.tile([P, ROW_TILES, WIDTH], F32, bufs=PRE_BUFS)
-            h_rows = work.tile([P, ROW_TILES, WORD_PAIRS, P, PAIR], BF16)
+            acc1_of[g] = []
             for r in range(ROW_TILES):
                 rows = slice(r * P, (r + 1) * P)
                 acc1 = banks.tile([P, WIDTH], F32, tag="bank")
@@ -165,20 +188,23 @@ def tile_linearwdecoder_pa_e_kernel(tc, z1, z2, W1_words, W1_scales, b1, W2_word
                     start=True,
                     stop=True,
                 )
-                nc.vector.tensor_tensor(out=pre[:, r, :], in0=acc1[:], in1=b1_spread[:, g, :], op=ADD)
-                nc.gpsimd.tensor_scalar(
-                    out=h_rows[:, r, :, :, :],
-                    in0=pre[:, r, :].rearrange("b (m u e) -> b u m e", u=WORD_PAIRS, e=PAIR),
-                    scalar1=1.0,
-                    scalar2=0.0,
-                    op0=MULT,
-                    op1=ADD,
-                )
+                acc1_of[g].append(acc1)
+
+        def add1(g):
+            pre = work.tile([P, ROW_TILES, WIDTH], F32, bufs=PRE_BUFS)
+            for r in range(ROW_TILES):
+                nc.vector.tensor_tensor(out=pre[:, r, :], in0=acc1_of[g][r][:], in1=b1_spread[:, g, :], op=ADD)
             pre_of[g] = pre
+
+        def round_hidden(g):
+            h_rows = work.tile([P, ROW_TILES, WORD_PAIRS, P, PAIR], BF16)
+            for r in range(ROW_TILES):
+                rounded = h_rows[:, r, :, :, :]
+                before = pre_of[g][:, r, :].rearrange("b (m u e) -> b u m e", u=WORD_PAIRS, e=PAIR)
+                nc.gpsimd.tensor_scalar(out=rounded, in0=before, scalar1=1.0, scalar2=0.0, op0=MULT, op1=ADD)
             h_rows_of[g] = h_rows
 
         def transpose_hidden(g):
-            h_grouped = work.tile([P, BATCH, PACK], BF16, align_bytes=64)
             h_bank = banks.tile([P, WORD_PAIRS, BATCH], F32, tag="bank")
             for r in range(ROW_TILES):
                 for u in range(WORD_PAIRS):
@@ -187,9 +213,13 @@ def tile_linearwdecoder_pa_e_kernel(tc, z1, z2, W1_words, W1_scales, b1, W2_word
                         h_rows_of[g][:, r, u, :, :].rearrange("b m e -> b (m e)").bitcast(F32),
                         ident_f32[:],
                     )
+            h_bank_of[g] = h_bank
+
+        def copy_hidden(g):
+            h_grouped = work.tile([P, BATCH, PACK], BF16, align_bytes=64)
             nc.scalar.activation(
                 out=h_grouped[:].rearrange("p b (u e) -> p b u e", u=WORD_PAIRS),
-                in_=h_bank[:].rearrange("p u b -> p (u b)").bitcast(BF16).rearrange("p (u b e) -> p b u e", u=WORD_PAIRS, e=PAIR),
+                in_=h_bank_of[g][:].rearrange("p u b -> p (u b)").bitcast(BF16).rearrange("p (u b e) -> p b u e", u=WORD_PAIRS, e=PAIR),
                 func=RELU,
             )
             h_grouped_of[g] = h_grouped
@@ -202,65 +232,73 @@ def tile_linearwdecoder_pa_e_kernel(tc, z1, z2, W1_words, W1_scales, b1, W2_word
             )
             h_quantised[g] = (h_words, h_plane)
 
-        def layer2(g):
+        def multiply2(g):
             h_words, h_plane = h_quantised[g]
-            branch = work.tile([P, COL_TILES, BATCH], F32)
+            acc2_of[g] = []
             for bank_no in range(COL_TILES // BANK_COL_TILES):
                 acc2 = banks.tile([P, BANK_COL_TILES, BATCH], F32, tag="bank")
                 for i in range(BANK_COL_TILES):
-                    j = BANK_COL_TILES * bank_no + i
+                    cols = slice((BANK_COL_TILES * bank_no + i) * P, (BANK_COL_TILES * bank_no + i + 1) * P)
                     nc.tensor.matmul_mx(
                         out=acc2[:, i, :],
-                        lhsT=w2_words[:, g, j * P : (j + 1) * P].bitcast(FP8X4),
-                        lhsT_scale=plane_of(w2_planes, g)[:, j * P : (j + 1) * P],
+                        lhsT=w2_words[:, g, cols].bitcast(FP8X4),
+                        lhsT_scale=plane_of(w2_planes, g)[:, cols],
                         rhs=h_words[:].bitcast(FP8X4),
                         rhs_scale=h_plane[:],
                         start=True,
                         stop=True,
                     )
-                for i in range(BANK_COL_TILES):
-                    j = BANK_COL_TILES * bank_no + i
-                    nc.scalar.activation(
-                        out=branch[:, j, :],
-                        in_=acc2[:, i, :],
-                        func=RELU,
-                        bias=b2_columns[:, COL_TILES * g + j : COL_TILES * g + j + 1],
-                    )
+                acc2_of[g].append(acc2)
+
+        def activate2(g):
+            branch = work.tile([P, COL_TILES, BATCH], F32)
+            for j in range(COL_TILES):
+                nc.scalar.activation(
+                    out=branch[:, j, :],
+                    in_=acc2_of[g][j // BANK_COL_TILES][:, j % BANK_COL_TILES, :],
+                    func=RELU,
+                    bias=b2_columns[:, COL_TILES * g + j : COL_TILES * g + j + 1],
+                )
             branch_of[g] = branch
+
+        def transpose_branch(g):
+            back_of[g] = []
+            for r in range(ROW_TILES):
+                back = banks.tile([P, WIDTH], F32, tag="bank")
+                for j in range(COL_TILES):
+                    nc.tensor.transpose(back[:, j * P : (j + 1) * P], branch_of[g][:, j, r * P : (r + 1) * P], ident_f32[:])
+                back_of[g].append(back)
 
         def finish(g):
             for r in range(ROW_TILES):
-                rows = slice(r * P, (r + 1) * P)
-                back = banks.tile([P, WIDTH], F32, tag="bank")
-                for j in range(COL_TILES):
-                    nc.tensor.transpose(back[:, j * P : (j + 1) * P], branch_of[g][:, j, rows], ident_f32[:])
                 result = work.tile([P, WIDTH], F32, bufs=RESULT_BUFS)
                 nc.vector.scalar_tensor_tensor(
-                    out=result[:],
-                    in0=pre_of[g][:, r, :],
-                    scalar=0.0,
-                    in1=back[:],
-                    op0=MAX,
-                    op1=ADD,
+                    out=result[:], in0=pre_of[g][:, r, :], scalar=0.0, in1=back_of[g][r][:], op0=MAX, op1=ADD
                 )
-                nc.sync.dma_start(out=out[rows, g, :], in_=result[:])
+                nc.sync.dma_start(out=out[r * P : (r + 1) * P, g, :], in_=result[:])
 
-
-        def in_flight(g):
-            return 0 <= g < CODES
-
-        for round_no in range(CODES + LAG_FINISH):
-            if in_flight(round_no):
-                quantise_z(round_no)
-            if in_flight(round_no - LAG_HIDDEN):
-                transpose_hidden(round_no - LAG_HIDDEN)
-            if in_flight(round_no - LAG_LAYER1):
-                layer1(round_no - LAG_LAYER1)
-            if in_flight(round_no - LAG_FINISH):
-                finish(round_no - LAG_FINISH)
-            if in_flight(round_no - LAG_HIDDEN):
-                quantise_hidden(round_no - LAG_HIDDEN)
-            if in_flight(round_no - LAG_LAYER2):
-                layer2(round_no - LAG_LAYER2)
-            if round_no < BIAS_ROUNDS:
-                spread_bias(round_no * BIAS_CODES)
+        steps = (
+            (transpose_z, 0),
+            (copy_z, 0),
+            (quantise_z, 0),
+            (transpose_hidden, 3),
+            (copy_hidden, 3),
+            (multiply1, 1),
+            (add1, 1),
+            (round_hidden, 1),
+            (transpose_branch, 7),
+            (finish, 7),
+            (quantise_hidden, 3),
+            (multiply2, 5),
+            (activate2, 5),
+        )
+        spread_bias(0)
+        spread_bias(2)
+        for round_no in range(ROUNDS):
+            for step, lag in steps:
+                if 0 <= round_no - lag < CODES:
+                    step(round_no - lag)
+            if round_no == 1:
+                columns_of_b2()
+            if 2 * round_no + 4 < CODES:
+                spread_bias(2 * round_no + 4)

@@ -135,7 +135,7 @@ def tile_linearwdecoder_pa_e_kernel(tc, z1, z2, W1_words, W1_scales, b1, W2_word
                     start=True,
                     stop=True,
                 )
-            nc.scalar.copy(out=b1_spread[:, first : first + BANK_BIASES, :], in_=bias_bank[:])
+            nc.vector.tensor_copy(out=b1_spread[:, first : first + BANK_BIASES, :], in_=bias_bank[:])
 
         z_pairs = z_rows[:].bitcast(F32)
         z_bank_of = {}
@@ -190,11 +190,29 @@ def tile_linearwdecoder_pa_e_kernel(tc, z1, z2, W1_words, W1_scales, b1, W2_word
                 )
                 acc1_of[g].append(acc1)
 
-        def add1(g):
-            pre = work.tile([P, ROW_TILES, WIDTH], F32, bufs=PRE_BUFS)
-            for r in range(ROW_TILES):
-                nc.vector.tensor_tensor(out=pre[:, r, :], in0=acc1_of[g][r][:], in1=b1_spread[:, g, :], op=ADD)
-            pre_of[g] = pre
+        def add1_of(g, r):
+            if r == 0:
+                pre_of[g] = work.tile([P, ROW_TILES, WIDTH], F32, bufs=PRE_BUFS, name="pre")
+            nc.vector.tensor_tensor(out=pre_of[g][:, r, :], in0=acc1_of[g][r][:], in1=b1_spread[:, g, :], op=ADD)
+
+        def add1a(g):
+            add1_of(g, 0)
+
+        def add1b(g):
+            add1_of(g, 1)
+
+        def finish_of(g, r):
+            result = work.tile([P, WIDTH], F32, bufs=RESULT_BUFS)
+            nc.vector.scalar_tensor_tensor(
+                out=result[:], in0=pre_of[g][:, r, :], scalar=0.0, in1=back_of[g][r][:], op0=MAX, op1=ADD
+            )
+            nc.sync.dma_start(out=out[r * P : (r + 1) * P, g, :], in_=result[:])
+
+        def finisha(g):
+            finish_of(g, 0)
+
+        def finishb(g):
+            finish_of(g, 1)
 
         def round_hidden(g):
             h_rows = work.tile([P, ROW_TILES, WORD_PAIRS, P, PAIR], BF16)
@@ -269,26 +287,20 @@ def tile_linearwdecoder_pa_e_kernel(tc, z1, z2, W1_words, W1_scales, b1, W2_word
                     nc.tensor.transpose(back[:, j * P : (j + 1) * P], branch_of[g][:, j, r * P : (r + 1) * P], ident_f32[:])
                 back_of[g].append(back)
 
-        def finish(g):
-            for r in range(ROW_TILES):
-                result = work.tile([P, WIDTH], F32, bufs=RESULT_BUFS)
-                nc.vector.scalar_tensor_tensor(
-                    out=result[:], in0=pre_of[g][:, r, :], scalar=0.0, in1=back_of[g][r][:], op0=MAX, op1=ADD
-                )
-                nc.sync.dma_start(out=out[r * P : (r + 1) * P, g, :], in_=result[:])
-
         steps = (
             (transpose_z, 0),
             (copy_z, 0),
-            (quantise_z, 0),
             (transpose_hidden, 3),
             (copy_hidden, 3),
             (multiply1, 1),
-            (add1, 1),
-            (round_hidden, 1),
             (transpose_branch, 7),
-            (finish, 7),
+            (add1a, 1),
+            (quantise_z, 0),
+            (add1b, 1),
+            (finisha, 7),
+            (finishb, 7),
             (quantise_hidden, 3),
+            (round_hidden, 1),
             (multiply2, 5),
             (activate2, 5),
         )

from contextlib import ExitStack

import concourse.mybir as mybir
from concourse.masks import make_identity

F32 = mybir.dt.float32
BF16 = mybir.dt.bfloat16
I32 = mybir.dt.int32
U32 = mybir.dt.uint32
U8 = mybir.dt.uint8
FP8X4 = mybir.dt.float8_e4m3fn_x4
RELU = mybir.ActivationFunctionType.Relu
ADD = mybir.AluOpType.add
MAX = mybir.AluOpType.max
MULT = mybir.AluOpType.mult

P = 128
PACK = 4
BATCH = 256
ROW_TILES = BATCH // P
CODES = 16
HALF = 256
WIDTH = 2 * HALF
PAIRS = WIDTH // 2
COL_TILES = WIDTH // P
QUADRANT = 32
LIVE = 4
PLANES = 4
BANK_BYTES = 2048
PAIR = 2
WORD_PAIRS = PACK // PAIR
BANK_BIASES = BANK_BYTES // (2 * WIDTH)
BANK_COL_TILES = BANK_BYTES // (4 * BATCH)

FLOPS = 2 * 2 * BATCH * CODES * WIDTH * WIDTH

STEP_BUFS = 4
PRE_BUFS = 8
RESULT_BUFS = 16
PSUM_BANKS = 8
LOAD_CODES = 2
W2_LAG = 4
ROUNDS = CODES + 7


def tile_linearwdecoder_pa_e_kernel(tc, z1, z2, W1_words, W1_scales, b1, W2_words, W2_scales, b2, out):
    nc = tc.nc
    with ExitStack() as stack:
        resident = stack.enter_context(tc.tile_pool(name="resident", bufs=1))
        work = stack.enter_context(tc.tile_pool(name="work", bufs=STEP_BUFS))
        banks = stack.enter_context(tc.psum_pool(name="banks", bufs=PSUM_BANKS))
        stack.enter_context(tc.manual_schedule())

        z_rows = resident.tile([P, ROW_TILES, CODES, WIDTH], BF16)
        w1_words = resident.tile([P, CODES, WIDTH], U32, align_bytes=64)
        w2_words = resident.tile([P, CODES, WIDTH], U32, align_bytes=64)
        w1_planes = resident.tile([P, CODES // PLANES, WIDTH], U8, align_bytes=64)
        w2_planes = resident.tile([P, CODES // PLANES, WIDTH], U8, align_bytes=64)
        b1_by_code = resident.tile([P, WIDTH], BF16)
        b1_spread = resident.tile([P, CODES, WIDTH], BF16)
        b2_by_tile = resident.tile([P, P], BF16)
        b2_columns = resident.tile([P, CODES * COL_TILES], F32)
        ident_f32 = resident.tile([P, P], F32)
        ident_bf16 = resident.tile([P, P], BF16)

        nc.vector.memset(b1_by_code[:], 0.0)
        nc.vector.memset(w1_planes[:].rearrange("p a n -> p (a n)").bitcast(I32), 0)
        nc.vector.memset(b2_by_tile[:], 0.0)
        nc.vector.memset(w2_planes[:].rearrange("p a n -> p (a n)").bitcast(I32), 0)
        make_identity(nc, ident_bf16[:])
        make_identity(nc, ident_f32[:])


        def load_planes(planes, scales, group):
            for quadrant in range(P // QUADRANT):
                nc.sync.dma_start(
                    out=planes[QUADRANT * quadrant : QUADRANT * quadrant + LIVE * PLANES, group, :].bitcast(I32),
                    in_=scales[PLANES * group : PLANES * (group + 1), LIVE * quadrant : LIVE * (quadrant + 1), :].bitcast(I32),
                )

        def load_words(words, packed, first, count):
            codes = slice(first, first + count)
            nc.sync.dma_start(
                out=words[:, codes, :].bitcast(I32), in_=packed[codes].rearrange("g p n t -> p g (n t)").bitcast(I32)
            )

        def load_z(first, count):
            codes = slice(first, first + count)
            z_cols = slice(first * HALF, (first + count) * HALF)
            for r in range(ROW_TILES):
                rows = slice(r * P, (r + 1) * P)
                for half, z in enumerate((z1, z2)):
                    nc.sync.dma_start(
                        out=z_rows[:, r, codes, half * HALF : (half + 1) * HALF],
                        in_=z[rows, z_cols].rearrange("b (g k) -> b g k", k=HALF),
                    )

        def load_b1():
            nc.sync.dma_start(out=b1_by_code[0:CODES, :], in_=b1)

        def load_b2():
            nc.sync.dma_start(out=b2_by_tile[0 : CODES * COL_TILES, :], in_=b2.rearrange("g (j m) -> (g j) m", m=P))

        load_b1()
        for first in range(0, CODES + W2_LAG, LOAD_CODES):
            if first < CODES:
                load_z(first, LOAD_CODES)
                if first % PLANES == 0:
                    load_planes(w1_planes, W1_scales, first // PLANES)
                load_words(w1_words, W1_words, first, LOAD_CODES)
            if first == 0:
                load_b2()
            late = first - W2_LAG
            if late >= 0:
                if late % PLANES == 0:
                    load_planes(w2_planes, W2_scales, late // PLANES)
                load_words(w2_words, W2_words, late, LOAD_CODES)

        def plane_of(planes, g):
            return planes[LIVE * (g % PLANES) : P, g // PLANES, :]


        def columns_of_b2():
            b2_bank = banks.tile([P, BANK_BYTES // 2], BF16, tag="bank")
            nc.tensor.transpose(b2_bank[:, 0:P], b2_by_tile[:], ident_bf16[:])
            nc.vector.tensor_copy(out=b2_columns[:], in_=b2_bank[:, 0 : CODES * COL_TILES])

        def spread_bias(first):
            bias_bank = banks.tile([P, BANK_BIASES, WIDTH], BF16, tag="bank")
            for i in range(BANK_BIASES):
                nc.tensor.matmul(
                    out=bias_bank[:, i, :],
                    lhsT=ident_bf16[:, first + i : first + i + 1].to_broadcast([P, P]),
                    rhs=b1_by_code[:],
                    start=True,
                    stop=True,
                )
            nc.vector.tensor_copy(out=b1_spread[:, first : first + BANK_BIASES, :], in_=bias_bank[:])

        z_pairs = z_rows[:].bitcast(F32)
        z_bank_of = {}
        z_grouped_of = {}
        z_quantised = {}
        acc1_of = {}
        pre_of = {}
        h_rows_of = {}
        h_bank_of = {}
        h_grouped_of = {}
        h_quantised = {}
        acc2_of = {}
        branch_of = {}
        back_of = {}

        def transpose_z(g):
            z_bank = banks.tile([P, WORD_PAIRS, BATCH], F32, tag="bank")
            for r in range(ROW_TILES):
                for u in range(WORD_PAIRS):
                    nc.tensor.transpose(
                        z_bank[:, u, r * P : (r + 1) * P], z_pairs[:, r, g, u:PAIRS:WORD_PAIRS], ident_f32[:]
                    )
            z_bank_of[g] = z_bank

        def copy_z(g):
            z_grouped = work.tile([P, BATCH, PACK], BF16, align_bytes=64)
            nc.scalar.copy(out=z_grouped[:].bitcast(F32), in_=z_bank_of[g][:].rearrange("p u b -> p b u"))
            z_grouped_of[g] = z_grouped

        def quantise_z(g):
            z_words = work.tile([P, BATCH], U32, align_bytes=64)
            z_plane = work.tile([P, BATCH], U8, align_bytes=64)
            nc.vector.quantize_mx(
                out=z_words[:].bitcast(FP8X4), scales=z_plane[:], in_=z_grouped_of[g][:].rearrange("p b t -> p (b t)")
            )
            z_quantised[g] = (z_words, z_plane)

        def multiply1(g):
            z_words, z_plane = z_quantised[g]
            acc1_of[g] = []
            for r in range(ROW_TILES):
                rows = slice(r * P, (r + 1) * P)
                acc1 = banks.tile([P, WIDTH], F32, tag="bank")
                nc.tensor.matmul_mx(
                    out=acc1[:],
                    lhsT=z_words[:, rows].bitcast(FP8X4),
                    lhsT_scale=z_plane[:, rows],
                    rhs=w1_words[:, g, :].bitcast(FP8X4),
                    rhs_scale=plane_of(w1_planes, g),
                    start=True,
                    stop=True,
                )
                acc1_of[g].append(acc1)

        def add1_of(g, r):
            if r == 0:
                pre_of[g] = work.tile([P, ROW_TILES, WIDTH], F32, bufs=PRE_BUFS, name="pre")
            nc.vector.tensor_tensor(out=pre_of[g][:, r, :], in0=acc1_of[g][r][:], in1=b1_spread[:, g, :], op=ADD)

        def add1a(g):
            add1_of(g, 0)

        def add1b(g):
            add1_of(g, 1)

        def finish_of(g, r):
            result = work.tile([P, WIDTH], F32, bufs=RESULT_BUFS)
            nc.vector.scalar_tensor_tensor(
                out=result[:], in0=pre_of[g][:, r, :], scalar=0.0, in1=back_of[g][r][:], op0=MAX, op1=ADD
            )
            nc.sync.dma_start(out=out[r * P : (r + 1) * P, g, :], in_=result[:])

        def finisha(g):
            finish_of(g, 0)

        def finishb(g):
            finish_of(g, 1)

        def round_hidden(g):
            h_rows = work.tile([P, ROW_TILES, WORD_PAIRS, P, PAIR], BF16)
            for r in range(ROW_TILES):
                rounded = h_rows[:, r, :, :, :]
                before = pre_of[g][:, r, :].rearrange("b (m u e) -> b u m e", u=WORD_PAIRS, e=PAIR)
                nc.gpsimd.tensor_scalar(out=rounded, in0=before, scalar1=1.0, scalar2=0.0, op0=MULT, op1=ADD)
            h_rows_of[g] = h_rows

        def transpose_hidden(g):
            h_bank = banks.tile([P, WORD_PAIRS, BATCH], F32, tag="bank")
            for r in range(ROW_TILES):
                for u in range(WORD_PAIRS):
                    nc.tensor.transpose(
                        h_bank[:, u, r * P : (r + 1) * P],
                        h_rows_of[g][:, r, u, :, :].rearrange("b m e -> b (m e)").bitcast(F32),
                        ident_f32[:],
                    )
            h_bank_of[g] = h_bank

        def copy_hidden(g):
            h_grouped = work.tile([P, BATCH, PACK], BF16, align_bytes=64)
            nc.scalar.activation(
                out=h_grouped[:].rearrange("p b (u e) -> p b u e", u=WORD_PAIRS),
                in_=h_bank_of[g][:].rearrange("p u b -> p (u b)").bitcast(BF16).rearrange("p (u b e) -> p b u e", u=WORD_PAIRS, e=PAIR),
                func=RELU,
            )
            h_grouped_of[g] = h_grouped

        def quantise_hidden(g):
            h_words = work.tile([P, BATCH], U32, align_bytes=64)
            h_plane = work.tile([P, BATCH], U8, align_bytes=64)
            nc.vector.quantize_mx(
                out=h_words[:].bitcast(FP8X4), scales=h_plane[:], in_=h_grouped_of[g][:].rearrange("p b t -> p (b t)")
            )
            h_quantised[g] = (h_words, h_plane)

        def multiply2(g):
            h_words, h_plane = h_quantised[g]
            acc2_of[g] = []
            for bank_no in range(COL_TILES // BANK_COL_TILES):
                acc2 = banks.tile([P, BANK_COL_TILES, BATCH], F32, tag="bank")
                for i in range(BANK_COL_TILES):
                    cols = slice((BANK_COL_TILES * bank_no + i) * P, (BANK_COL_TILES * bank_no + i + 1) * P)
                    nc.tensor.matmul_mx(
                        out=acc2[:, i, :],
                        lhsT=w2_words[:, g, cols].bitcast(FP8X4),
                        lhsT_scale=plane_of(w2_planes, g)[:, cols],
                        rhs=h_words[:].bitcast(FP8X4),
                        rhs_scale=h_plane[:],
                        start=True,
                        stop=True,
                    )
                acc2_of[g].append(acc2)

        def activate2(g):
            branch = work.tile([P, COL_TILES, BATCH], F32)
            for j in range(COL_TILES):
                nc.scalar.activation(
                    out=branch[:, j, :],
                    in_=acc2_of[g][j // BANK_COL_TILES][:, j % BANK_COL_TILES, :],
                    func=RELU,
                    bias=b2_columns[:, COL_TILES * g + j : COL_TILES * g + j + 1],
                )
            branch_of[g] = branch

        def transpose_branch(g):
            back_of[g] = []
            for r in range(ROW_TILES):
                back = banks.tile([P, WIDTH], F32, tag="bank")
                for j in range(COL_TILES):
                    nc.tensor.transpose(back[:, j * P : (j + 1) * P], branch_of[g][:, j, r * P : (r + 1) * P], ident_f32[:])
                back_of[g].append(back)

        steps = (
            (transpose_z, 0),
            (copy_z, 0),
            (transpose_hidden, 3),
            (copy_hidden, 3),
            (multiply1, 1),
            (transpose_branch, 7),
            (add1a, 1),
            (quantise_z, 0),
            (add1b, 1),
            (finisha, 7),
            (finishb, 7),
            (quantise_hidden, 3),
            (round_hidden, 1),
            (multiply2, 5),
            (activate2, 5),
        )
        spread_bias(0)
        spread_bias(2)
        for round_no in range(ROUNDS):
            for step, lag in steps:
                if 0 <= round_no - lag < CODES:
                    step(round_no - lag)
            if round_no == 1:
                columns_of_b2()
            if 2 * round_no + 4 < CODES:
                spread_bias(2 * round_no + 4)
